import numpy as np
import ml_dtypes


def mxq(x, axis, fmt="e4m3"):
    dtype, down = {"e4m3": (ml_dtypes.float8_e4m3fn, 7), "e5m2": (ml_dtypes.float8_e5m2, 14)}[fmt]
    v = np.moveaxis(np.asarray(x, np.float32).astype(ml_dtypes.bfloat16).astype(np.float64), axis, -1)
    blocks = v.reshape(v.shape[:-1] + (-1, 32))
    amax = np.abs(blocks).max(-1, keepdims=True)
    byte = np.maximum(np.where(amax > 0, np.frexp(amax)[1] - 1 + 127, 0) - down, 1)
    scale = np.exp2(byte - 127.0)
    codes = (blocks / scale).astype(np.float32).astype(dtype).astype(np.float64)
    return np.moveaxis((codes * scale).reshape(v.shape), -1, axis)


WIDE = False


def mx_kscale(k):
    if not WIDE:
        return np.ones(k)
    levels = np.array([10, -10, 5, -5, 0])
    a = np.random.permutation(np.resize(levels, k // 512 * 4)).reshape(k // 512, 4)
    idx = np.arange(k)
    return np.exp2(a[idx // 512, idx % 128 // 32])


BF16 = ml_dtypes.bfloat16


def bf(x):
    return np.asarray(x, np.float32).astype(BF16)


def f64(x):
    return np.asarray(x).astype(np.float64)


S, D, H, HD, CQ, CKV, O = 4096, 512, 6, 128, 96, 512, 2048
E = H * HD
ROPE_BASE = 10000.0


def rope(xh, cos, sin):
    half = xh.shape[-1] // 2
    x1, x2 = xh[..., :half], xh[..., half:]
    rot = np.concatenate([-x2, x1], axis=-1)
    return xh * cos[:, None, :] + rot * sin[:, None, :]


def setup_inputs():
    s, t = mx_kscale(D), mx_kscale(CKV)
    pos = np.arange(S, dtype=np.float64)[:, None]
    inv_freq = 1.0 / (ROPE_BASE ** (np.arange(0, HD, 2, dtype=np.float64) / HD))
    ang = pos * inv_freq[None, :]
    return {"x": bf(np.random.standard_normal((S, D)) * s[None, :]),
            "rope_cos": bf(np.concatenate([np.cos(ang), np.cos(ang)], axis=-1)),
            "rope_sin": bf(np.concatenate([np.sin(ang), np.sin(ang)], axis=-1)),
            "wkv_down": bf(np.random.standard_normal((CKV, D)) / np.sqrt(D) * t[:, None] / s[None, :]),
            "bkv_down": bf(np.random.standard_normal(CKV) * 0.3 * t),
            "wk_up": bf(np.random.standard_normal((E, CKV)) / np.sqrt(CKV) / t[None, :]),
            "bk_up": bf(np.random.standard_normal(E) * 0.3),
            "wv_up": bf(np.random.standard_normal((E, CKV)) / np.sqrt(CKV) / t[None, :]),
            "bv_up": bf(np.random.standard_normal(E) * 0.3)}


def reference(x, rope_cos, rope_sin, wkv_down, bkv_down, wk_up, bk_up, wv_up, bv_up):
    c_kv = (mxq(f64(x), 1, "e4m3") @ mxq(f64(wkv_down), 1, "e4m3").T) + f64(bkv_down)
    cq = mxq(c_kv, 1, "e4m3")
    k = ((cq @ mxq(f64(wk_up), 1, "e4m3").T) + f64(bk_up)).reshape(S, H, HD)
    v = ((cq @ mxq(f64(wv_up), 1, "e4m3").T) + f64(bv_up)).reshape(S, H, HD)
    return rope(k, f64(rope_cos), f64(rope_sin)), v

@@ -1,0 +1,306 @@
+from contextlib import ExitStack
+
+import concourse.mybir as mybir
+from concourse.masks import make_identity
+
+F32 = mybir.dt.float32
+BF16 = mybir.dt.bfloat16
+U32 = mybir.dt.uint32
+U8 = mybir.dt.uint8
+FP8X4 = mybir.dt.float8_e4m3fn_x4
+ADD = mybir.AluOpType.add
+MULT = mybir.AluOpType.mult
+IDENTITY = mybir.ActivationFunctionType.Identity
+
+P = 128
+TOKENS = 4096
+K = 512
+HEADS = 6
+HEAD = 128
+HALF = HEAD // 2
+E = HEADS * HEAD
+BANK = 512
+TILES = TOKENS // P
+BLOCK_TILES = 4
+BLOCK = BLOCK_TILES * P
+BLOCKS = TILES // BLOCK_TILES
+BLOCK_OUT = BLOCK_TILES * E
+
+FLOPS = 2 * TOKENS * K * (K + 2 * E)
+
+
+def tile_selfattention_pa_t_kernel(
+    tc, x, rope_cos, rope_sin, wkv_down, bkv_down, wk_up, bk_up, wv_up, bv_up, out_0, out_1
+):
+    nc = tc.nc
+    with ExitStack() as stack:
+        consts = stack.enter_context(tc.tile_pool(name="consts", bufs=1))
+        rows = stack.enter_context(tc.tile_pool(name="rows", bufs=1))
+        weights = stack.enter_context(tc.tile_pool(name="weights", bufs=1))
+        stage = stack.enter_context(tc.tile_pool(name="stage", bufs=3))
+        pairs = stack.enter_context(tc.tile_pool(name="pairs", bufs=2))
+        s_banks = stack.enter_context(tc.psum_pool(name="s_banks", bufs=4))
+        v_banks = stack.enter_context(tc.psum_pool(name="v_banks", bufs=4))
+        stack.enter_context(tc.manual_schedule())
+
+        x_dram = x.rearrange("(p t) d -> p t d", t=TILES)
+        cos_dram = rope_cos.rearrange("(p t) j -> p t j", t=TILES)
+        sin_dram = rope_sin.rearrange("(p t) j -> p t j", t=TILES)
+        k_dram = out_0.rearrange("(p t) h j -> p (t h j)", t=TILES)
+        v_dram = out_1.rearrange("(p t) h j -> p (t h j)", t=TILES)
+
+        x_rows = rows.tile([P, TILES, K], BF16)
+        cos_rows = rows.tile([P, TILES, HEAD], BF16)
+        sin_rows = rows.tile([P, TILES, HEAD], BF16)
+        sin_rot = rows.tile([P, TILES, HEAD], BF16)
+        down_rows = rows.tile([P, 4, K], BF16)
+        up_rows = rows.tile([P, 2 * HEADS, K], BF16)
+        bkv_bf = consts.tile([P, 4], BF16)
+        bk_bf = consts.tile([P, HEADS], BF16)
+        bv_bf = consts.tile([P, E], BF16)
+
+        def load_block(b):
+            t_range = slice(b * BLOCK_TILES, (b + 1) * BLOCK_TILES)
+            nc.sync.dma_start(out=x_rows[:, t_range, :], in_=x_dram[:, t_range, :])
+            nc.sync.dma_start(out=cos_rows[:, t_range, :], in_=cos_dram[:, t_range, :])
+            nc.sync.dma_start(out=sin_rows[:, t_range, :], in_=sin_dram[:, t_range, :])
+
+        nc.sync.dma_start(
+            out=down_rows[:].rearrange("m (u e) d -> m u (e d)", u=2),
+            in_=wkv_down.rearrange("(u m e) d -> m u (e d)", u=2, e=2),
+        )
+        load_block(0)
+        nc.sync.dma_start(
+            out=bkv_bf[:].rearrange("m (u e) -> m u e", u=2),
+            in_=bkv_down.rearrange("(u m e) -> m u e", u=2, e=2),
+        )
+        nc.sync.dma_start(out=up_rows[:, 0:HEADS, :], in_=wk_up.rearrange("(a m) c -> m a c", m=P))
+        with nc.allow_non_contiguous_dma(reason="768 bias values, one head to a column"):
+            nc.sync.dma_start(out=bk_bf[:], in_=bk_up.rearrange("(h m) -> m h", m=P))
+        nc.sync.dma_start(
+            out=up_rows[:, HEADS : 2 * HEADS, :], in_=wv_up.rearrange("(a m) c -> m a c", m=P)
+        )
+        nc.sync.dma_start(out=bv_bf[:], in_=bv_up.partition_broadcast(P))
+        for b in range(1, BLOCKS):
+            load_block(b)
+
+        ident_f32 = consts.tile([P, P], F32)
+        make_identity(nc, ident_f32[:])
+        ident_bf = consts.tile([P, P], BF16)
+        make_identity(nc, ident_bf[:])
+        swap_f32 = consts.tile([P, P], F32)
+        nc.vector.tensor_copy(out=swap_f32[:, 0:HALF], in_=ident_f32[:, HALF:HEAD])
+        nc.vector.tensor_copy(out=swap_f32[:, HALF:HEAD], in_=ident_f32[:, 0:HALF])
+        bkv_col = consts.tile([P, 4], F32)
+        bk_col = consts.tile([P, HEADS], F32)
+        bv_twice = consts.tile([P, 2, E], F32)
+
+        down_codes = weights.tile([P, K], U32, align_bytes=64)
+        down_scales = weights.tile([P, K], U8, align_bytes=64)
+        up_codes = weights.tile([P, 2 * E], U32, align_bytes=64)
+        up_scales = weights.tile([P, 2 * E], U8, align_bytes=64)
+
+        def words_to_partitions(four_tiles, banks, copy):
+            grouped = stage.tile([P, 4 * BLOCK], BF16, align_bytes=64)
+            words_in = four_tiles.bitcast(F32)
+            words_out = grouped[:].bitcast(F32).rearrange("p (r n u) -> p r n u", r=4, u=2)
+            for first in (0, 2):
+                bank = banks.tile([P, 2, 2, P], F32, tag="bank")
+                for r in range(2):
+                    for u in range(2):
+                        nc.tensor.transpose(
+                            bank[:, r, u, :], words_in[:, first + r, u * P : (u + 1) * P], ident_f32[:]
+                        )
+                copy(
+                    out=words_out[:, first : first + 2, :, :],
+                    in_=bank[:].rearrange("p r u n -> p r n u"),
+                )
+            return grouped
+
+        def quantise(grouped, codes, scales):
+            nc.vector.quantize_mx(out=codes.bitcast(FP8X4), scales=scales, in_=grouped[:])
+
+        x_grouped = {}
+        x_mx = {}
+        c_planes = {}
+        c_grouped = {}
+        c_mx = {}
+        tables = {}
+        products = {}
+
+        def x_words(b):
+            t_range = slice(b * BLOCK_TILES, (b + 1) * BLOCK_TILES)
+            x_grouped[b] = words_to_partitions(x_rows[:, t_range, :], s_banks, nc.scalar.copy)
+
+        def x_quantise(b):
+            x_codes = pairs.tile([P, BLOCK], U32, align_bytes=64)
+            x_scales = pairs.tile([P, BLOCK], U8, align_bytes=64)
+            quantise(x_grouped[b], x_codes[:], x_scales[:])
+            x_mx[b] = (x_codes, x_scales)
+
+        def ckv_matmuls(b):
+            x_codes, x_scales = x_mx[b]
+            planes = pairs.tile([P, 4, BLOCK], BF16)
+            for t in range(4):
+                cols = slice(t * P, (t + 1) * P)
+                bank = s_banks.tile([P, BLOCK], F32, tag="bank")
+                nc.tensor.matmul_mx(
+                    out=bank[:],
+                    lhsT=down_codes[:, cols].bitcast(FP8X4),
+                    lhsT_scale=down_scales[:, cols],
+                    rhs=x_codes[:].bitcast(FP8X4),
+                    rhs_scale=x_scales[:],
+                    start=True,
+                    stop=True,
+                )
+                nc.scalar.activation(
+                    out=planes[:, t, :], in_=bank[:], func=IDENTITY, bias=bkv_col[:, t : t + 1], scale=1.0
+                )
+            c_planes[b] = planes
+
+        def ckv_regroup(b):
+            grouped = stage.tile([P, 4 * BLOCK], BF16, align_bytes=64)
+            nc.vector.tensor_copy(
+                out=grouped[:].rearrange("p (c i t) -> p c t i", i=4, t=4),
+                in_=c_planes[b][:].rearrange("p t (c i) -> p c t i", i=4),
+            )
+            c_grouped[b] = grouped
+
+        def ckv_quantise(b):
+            c_codes = pairs.tile([P, BLOCK], U32, align_bytes=64)
+            c_scales = pairs.tile([P, BLOCK], U8, align_bytes=64)
+            quantise(c_grouped[b], c_codes[:], c_scales[:])
+            c_mx[b] = (c_codes, c_scales)
+
+        def rope_tables(b):
+            t_range = slice(b * BLOCK_TILES, (b + 1) * BLOCK_TILES)
+            nc.gpsimd.tensor_scalar(
+                out=sin_rot[:, t_range, 0:HALF], in0=sin_rows[:, t_range, HALF:HEAD],
+                scalar1=1.0, scalar2=0.0, op0=MULT, op1=ADD,
+            )
+            nc.gpsimd.tensor_scalar(
+                out=sin_rot[:, t_range, HALF:HEAD], in0=sin_rows[:, t_range, 0:HALF],
+                scalar1=-1.0, scalar2=0.0, op0=MULT, op1=ADD,
+            )
+            bank = s_banks.tile([P, 2, BLOCK_TILES, P], BF16, tag="bank")
+            for i in range(BLOCK_TILES):
+                nc.tensor.transpose(bank[:, 0, i, :], cos_rows[:, b * BLOCK_TILES + i, :], ident_bf[:])
+                nc.tensor.transpose(bank[:, 1, i, :], sin_rot[:, b * BLOCK_TILES + i, :], ident_bf[:])
+            table = pairs.tile([P, 2, BLOCK], BF16)
+            nc.scalar.copy(out=table[:], in_=bank[:].rearrange("p w i n -> p w (i n)"))
+            tables[b] = table
+
+        def k_products(b):
+            c_codes, c_scales = c_mx[b]
+            product = pairs.tile([P, HEADS, 2, BLOCK], F32)
+            for h in range(HEADS):
+                cols = slice(h * HEAD, (h + 1) * HEAD)
+                bank = v_banks.tile([P, BLOCK], F32, tag="bank")
+                nc.tensor.matmul_mx(
+                    out=bank[:],
+                    lhsT=up_codes[:, cols].bitcast(FP8X4),
+                    lhsT_scale=up_scales[:, cols],
+                    rhs=c_codes[:].bitcast(FP8X4),
+                    rhs_scale=c_scales[:],
+                    start=True,
+                    stop=True,
+                )
+                nc.vector.scalar_tensor_tensor(
+                    out=product[:, h, :, :],
+                    in0=bank[:].unsqueeze(1).to_broadcast([P, 2, BLOCK]),
+                    scalar=bk_col[:, h : h + 1],
+                    in1=tables[b][:],
+                    op0=ADD,
+                    op1=MULT,
+                )
+            products[b] = product
+
+        def k_back(b):
+            product = products[b]
+            k_out = pairs.tile([P, BLOCK_OUT], F32)
+            for q in range(BLOCK_OUT // BANK):
+                bank = s_banks.tile([P, 4, HEAD], F32, tag="bank")
+                for s in range(4):
+                    i, h = divmod(q * 4 + s, HEADS)
+                    toks = slice(i * P, (i + 1) * P)
+                    nc.tensor.matmul(
+                        out=bank[:, s, :], lhsT=product[:, h, 0, toks], rhs=ident_f32[:],
+                        is_transpose=True, start=True, stop=False,
+                    )
+                    nc.tensor.matmul(
+                        out=bank[:, s, :], lhsT=product[:, h, 1, toks], rhs=swap_f32[:],
+                        is_transpose=True, start=False, stop=True,
+                    )
+                nc.scalar.copy(
+                    out=k_out[:, q * BANK : (q + 1) * BANK], in_=bank[:].rearrange("p s j -> p (s j)")
+                )
+            nc.sync.dma_start(out=k_dram[:, b * BLOCK_OUT : (b + 1) * BLOCK_OUT], in_=k_out[:])
+
+        def v_block(b):
+            c_codes, c_scales = c_mx[b]
+            v_out = pairs.tile([P, BLOCK_OUT], F32)
+            bias = bv_twice[:].rearrange("p r e -> p (r e)")
+            for q in range(BLOCK_OUT // BANK):
+                bank = v_banks.tile([P, BANK], F32, tag="bank")
+                col = q * BANK
+                while col < (q + 1) * BANK:
+                    i, e0 = divmod(col, E)
+                    width = min(E - e0, (q + 1) * BANK - col)
+                    toks = slice(i * P, (i + 1) * P)
+                    w_cols = slice(E + e0, E + e0 + width)
+                    nc.tensor.matmul_mx(
+                        out=bank[:, col - q * BANK : col - q * BANK + width],
+                        lhsT=c_codes[:, toks].bitcast(FP8X4),
+                        lhsT_scale=c_scales[:, toks],
+                        rhs=up_codes[:, w_cols].bitcast(FP8X4),
+                        rhs_scale=up_scales[:, w_cols],
+                        start=True,
+                        stop=True,
+                    )
+                    col += width
+                nc.vector.tensor_tensor(
+                    out=v_out[:, q * BANK : (q + 1) * BANK],
+                    in0=bank[:],
+                    in1=bias[:, (q % 3) * BANK : (q % 3 + 1) * BANK],
+                    op=ADD,
+                )
+            nc.sync.dma_start(out=v_dram[:, b * BLOCK_OUT : (b + 1) * BLOCK_OUT], in_=v_out[:])
+
+        down_grouped = words_to_partitions(down_rows[:], v_banks, nc.vector.tensor_copy)
+        x_words(0)
+        quantise(down_grouped, down_codes[:], down_scales[:])
+        x_quantise(0)
+        nc.vector.tensor_copy(out=bkv_col[:], in_=bkv_bf[:])
+        ckv_matmuls(0)
+        for chunk in range(3):
+            up_grouped = words_to_partitions(
+                up_rows[:, 4 * chunk : 4 * chunk + 4, :], v_banks, nc.vector.tensor_copy
+            )
+            cols = slice(chunk * BLOCK, (chunk + 1) * BLOCK)
+            quantise(up_grouped, up_codes[:, cols], up_scales[:, cols])
+        nc.vector.tensor_copy(out=bk_col[:], in_=bk_bf[:])
+        nc.vector.tensor_copy(out=bv_twice[:], in_=bv_bf[:].unsqueeze(1).to_broadcast([P, 2, E]))
+        x_words(1)
+        rope_tables(0)
+        ckv_regroup(0)
+        x_quantise(1)
+        ckv_quantise(0)
+
+        for b in range(BLOCKS + 1):
+            if b + 1 < BLOCKS:
+                ckv_matmuls(b + 1)
+            if b < BLOCKS:
+                k_products(b)
+            if b + 2 < BLOCKS:
+                x_words(b + 2)
+            if b + 1 < BLOCKS:
+                rope_tables(b + 1)
+                ckv_regroup(b + 1)
+            if b + 2 < BLOCKS:
+                x_quantise(b + 2)
+            if b + 1 < BLOCKS:
+                ckv_quantise(b + 1)
+            if b >= 1:
+                k_back(b - 1)
+            if b < BLOCKS:
+                v_block(b)

@@ -59,30 +59,38 @@ def tile_selfattention_pa_t_kernel(
         bk_bf = consts.tile([P, HEADS], BF16)
         bv_bf = consts.tile([P, E], BF16)
 
-        def load_block(b):
-            t_range = slice(b * BLOCK_TILES, (b + 1) * BLOCK_TILES)
-            nc.sync.dma_start(out=x_rows[:, t_range, :], in_=x_dram[:, t_range, :])
-            nc.sync.dma_start(out=cos_rows[:, t_range, :], in_=cos_dram[:, t_range, :])
-            nc.sync.dma_start(out=sin_rows[:, t_range, :], in_=sin_dram[:, t_range, :])
+        def tiles_of(b):
+            return slice(b * BLOCK_TILES, (b + 1) * BLOCK_TILES)
+
+        def load_x(b):
+            nc.sync.dma_start(out=x_rows[:, tiles_of(b), :], in_=x_dram[:, tiles_of(b), :])
+
+        def load_rope(b):
+            nc.sync.dma_start(out=cos_rows[:, tiles_of(b), :], in_=cos_dram[:, tiles_of(b), :])
+            nc.sync.dma_start(out=sin_rows[:, tiles_of(b), :], in_=sin_dram[:, tiles_of(b), :])
 
         nc.sync.dma_start(
             out=down_rows[:].rearrange("m (u e) d -> m u (e d)", u=2),
             in_=wkv_down.rearrange("(u m e) d -> m u (e d)", u=2, e=2),
         )
-        load_block(0)
+        load_x(0)
+        load_x(1)
         nc.sync.dma_start(
             out=bkv_bf[:].rearrange("m (u e) -> m u e", u=2),
             in_=bkv_down.rearrange("(u m e) -> m u e", u=2, e=2),
         )
         nc.sync.dma_start(out=up_rows[:, 0:HEADS, :], in_=wk_up.rearrange("(a m) c -> m a c", m=P))
-        with nc.allow_non_contiguous_dma(reason="768 bias values, one head to a column"):
-            nc.sync.dma_start(out=bk_bf[:], in_=bk_up.rearrange("(h m) -> m h", m=P))
         nc.sync.dma_start(
             out=up_rows[:, HEADS : 2 * HEADS, :], in_=wv_up.rearrange("(a m) c -> m a c", m=P)
         )
+        load_rope(0)
+        with nc.allow_non_contiguous_dma(reason="768 bias values, one head to a column"):
+            nc.sync.dma_start(out=bk_bf[:], in_=bk_up.rearrange("(h m) -> m h", m=P))
         nc.sync.dma_start(out=bv_bf[:], in_=bv_up.partition_broadcast(P))
-        for b in range(1, BLOCKS):
-            load_block(b)
+        for b in range(2, BLOCKS):
+            load_x(b)
+            load_rope(b - 1)
+        load_rope(BLOCKS - 1)
 
         ident_f32 = consts.tile([P, P], F32)
         make_identity(nc, ident_f32[:])
@@ -91,6 +99,15 @@ def tile_selfattention_pa_t_kernel(
         swap_f32 = consts.tile([P, P], F32)
         nc.vector.tensor_copy(out=swap_f32[:, 0:HALF], in_=ident_f32[:, HALF:HEAD])
         nc.vector.tensor_copy(out=swap_f32[:, HALF:HEAD], in_=ident_f32[:, 0:HALF])
+        for b in range(BLOCKS):
+            nc.gpsimd.tensor_scalar(
+                out=sin_rot[:, tiles_of(b), 0:HALF], in0=sin_rows[:, tiles_of(b), HALF:HEAD],
+                scalar1=1.0, scalar2=0.0, op0=MULT, op1=ADD,
+            )
+            nc.gpsimd.tensor_scalar(
+                out=sin_rot[:, tiles_of(b), HALF:HEAD], in0=sin_rows[:, tiles_of(b), 0:HALF],
+                scalar1=-1.0, scalar2=0.0, op0=MULT, op1=ADD,
+            )
         bkv_col = consts.tile([P, 4], F32)
         bk_col = consts.tile([P, HEADS], F32)
         bv_twice = consts.tile([P, 2, E], F32)
@@ -129,8 +146,7 @@ def tile_selfattention_pa_t_kernel(
         products = {}
 
         def x_words(b):
-            t_range = slice(b * BLOCK_TILES, (b + 1) * BLOCK_TILES)
-            x_grouped[b] = words_to_partitions(x_rows[:, t_range, :], s_banks, nc.scalar.copy)
+            x_grouped[b] = words_to_partitions(x_rows[:, tiles_of(b), :], s_banks, nc.scalar.copy)
 
         def x_quantise(b):
             x_codes = pairs.tile([P, BLOCK], U32, align_bytes=64)
@@ -173,15 +189,6 @@ def tile_selfattention_pa_t_kernel(
             c_mx[b] = (c_codes, c_scales)
 
         def rope_tables(b):
-            t_range = slice(b * BLOCK_TILES, (b + 1) * BLOCK_TILES)
-            nc.gpsimd.tensor_scalar(
-                out=sin_rot[:, t_range, 0:HALF], in0=sin_rows[:, t_range, HALF:HEAD],
-                scalar1=1.0, scalar2=0.0, op0=MULT, op1=ADD,
-            )
-            nc.gpsimd.tensor_scalar(
-                out=sin_rot[:, t_range, HALF:HEAD], in0=sin_rows[:, t_range, 0:HALF],
-                scalar1=-1.0, scalar2=0.0, op0=MULT, op1=ADD,
-            )
             bank = s_banks.tile([P, 2, BLOCK_TILES, P], BF16, tag="bank")
             for i in range(BLOCK_TILES):
                 nc.tensor.transpose(bank[:, 0, i, :], cos_rows[:, b * BLOCK_TILES + i, :], ident_bf[:])
@@ -190,10 +197,13 @@ def tile_selfattention_pa_t_kernel(
             nc.scalar.copy(out=table[:], in_=bank[:].rearrange("p w i n -> p w (i n)"))
             tables[b] = table
 
-        def k_products(b):
+        def k_products(b, heads):
             c_codes, c_scales = c_mx[b]
-            product = pairs.tile([P, HEADS, 2, BLOCK], F32)
-            for h in range(HEADS):
+            if b not in products:
+                product = pairs.tile([P, HEADS, 2, BLOCK], F32)
+                products[b] = product
+            product = products[b]
+            for h in heads:
                 cols = slice(h * HEAD, (h + 1) * HEAD)
                 bank = v_banks.tile([P, BLOCK], F32, tag="bank")
                 nc.tensor.matmul_mx(
@@ -213,27 +223,24 @@ def tile_selfattention_pa_t_kernel(
                     op0=ADD,
                     op1=MULT,
                 )
-            products[b] = product
 
         def k_back(b):
             product = products[b]
             k_out = pairs.tile([P, BLOCK_OUT], F32)
-            for q in range(BLOCK_OUT // BANK):
-                bank = s_banks.tile([P, 4, HEAD], F32, tag="bank")
-                for s in range(4):
-                    i, h = divmod(q * 4 + s, HEADS)
+            by_head = k_out[:].rearrange("p (i h j) -> p i h j", h=HEADS, j=HEAD)
+            for h in range(HEADS):
+                bank = s_banks.tile([P, BLOCK_TILES, HEAD], F32, tag="bank")
+                for i in range(BLOCK_TILES):
                     toks = slice(i * P, (i + 1) * P)
                     nc.tensor.matmul(
-                        out=bank[:, s, :], lhsT=product[:, h, 0, toks], rhs=ident_f32[:],
+                        out=bank[:, i, :], lhsT=product[:, h, 0, toks], rhs=ident_f32[:],
                         is_transpose=True, start=True, stop=False,
                     )
                     nc.tensor.matmul(
-                        out=bank[:, s, :], lhsT=product[:, h, 1, toks], rhs=swap_f32[:],
+                        out=bank[:, i, :], lhsT=product[:, h, 1, toks], rhs=swap_f32[:],
                         is_transpose=True, start=False, stop=True,
                     )
-                nc.scalar.copy(
-                    out=k_out[:, q * BANK : (q + 1) * BANK], in_=bank[:].rearrange("p s j -> p (s j)")
-                )
+                nc.scalar.copy(out=by_head[:, :, h, :], in_=bank[:])
             nc.sync.dma_start(out=k_dram[:, b * BLOCK_OUT : (b + 1) * BLOCK_OUT], in_=k_out[:])
 
         def v_block(b):
@@ -241,7 +248,8 @@ def tile_selfattention_pa_t_kernel(
             v_out = pairs.tile([P, BLOCK_OUT], F32)
             bias = bv_twice[:].rearrange("p r e -> p (r e)")
             for q in range(BLOCK_OUT // BANK):
-                bank = v_banks.tile([P, BANK], F32, tag="bank")
+                on_vector = q % 3 == 0
+                bank = (v_banks if on_vector else s_banks).tile([P, BANK], F32, tag="bank")
                 col = q * BANK
                 while col < (q + 1) * BANK:
                     i, e0 = divmod(col, E)
@@ -258,43 +266,54 @@ def tile_selfattention_pa_t_kernel(
                         stop=True,
                     )
                     col += width
-                nc.vector.tensor_tensor(
-                    out=v_out[:, q * BANK : (q + 1) * BANK],
-                    in0=bank[:],
-                    in1=bias[:, (q % 3) * BANK : (q % 3 + 1) * BANK],
-                    op=ADD,
-                )
-            nc.sync.dma_start(out=v_dram[:, b * BLOCK_OUT : (b + 1) * BLOCK_OUT], in_=v_out[:])
+                if on_vector:
+                    nc.vector.tensor_tensor(
+                        out=v_out[:, q * BANK : (q + 1) * BANK], in0=bank[:], in1=bias[:, 0:BANK], op=ADD
+                    )
+                else:
+                    nc.scalar.copy(out=v_out[:, q * BANK : (q + 1) * BANK], in_=bank[:])
+                if q % 3 == 2:
+                    two_banks = slice((q - 1) * BANK, (q + 1) * BANK)
+                    nc.gpsimd.tensor_tensor(
+                        out=v_out[:, two_banks], in0=v_out[:, two_banks], in1=bias[:, BANK : 3 * BANK], op=ADD
+                    )
+                    three_banks = slice((q - 2) * BANK, (q + 1) * BANK)
+                    nc.sync.dma_start(
+                        out=v_dram[:, b * BLOCK_OUT + (q - 2) * BANK : b * BLOCK_OUT + (q + 1) * BANK],
+                        in_=v_out[:, three_banks],
+                    )
 
-        down_grouped = words_to_partitions(down_rows[:], v_banks, nc.vector.tensor_copy)
-        x_words(0)
-        quantise(down_grouped, down_codes[:], down_scales[:])
-        x_quantise(0)
-        nc.vector.tensor_copy(out=bkv_col[:], in_=bkv_bf[:])
-        ckv_matmuls(0)
-        for chunk in range(3):
-            up_grouped = words_to_partitions(
-                up_rows[:, 4 * chunk : 4 * chunk + 4, :], v_banks, nc.vector.tensor_copy
-            )
+        def down_weights():
+            grouped = words_to_partitions(down_rows[:], v_banks, nc.vector.tensor_copy)
+            quantise(grouped, down_codes[:], down_scales[:])
+            nc.vector.tensor_copy(out=bkv_col[:], in_=bkv_bf[:])
+
+        def up_weights(chunk, banks, copy):
+            grouped = words_to_partitions(up_rows[:, 4 * chunk : 4 * chunk + 4, :], banks, copy)
             cols = slice(chunk * BLOCK, (chunk + 1) * BLOCK)
-            quantise(up_grouped, up_codes[:, cols], up_scales[:, cols])
-        nc.vector.tensor_copy(out=bk_col[:], in_=bk_bf[:])
-        nc.vector.tensor_copy(out=bv_twice[:], in_=bv_bf[:].unsqueeze(1).to_broadcast([P, 2, E]))
+            quantise(grouped, up_codes[:, cols], up_scales[:, cols])
+
+        down_weights()
+        x_words(0)
+        x_quantise(0)
         x_words(1)
-        rope_tables(0)
+        up_weights(0, v_banks, nc.vector.tensor_copy)
+        ckv_matmuls(0)
+        up_weights(1, v_banks, nc.vector.tensor_copy)
         ckv_regroup(0)
         x_quantise(1)
         ckv_quantise(0)
+        up_weights(2, s_banks, nc.scalar.copy)
+        nc.vector.tensor_copy(out=bk_col[:], in_=bk_bf[:])
+        nc.vector.tensor_copy(out=bv_twice[:], in_=bv_bf[:].unsqueeze(1).to_broadcast([P, 2, E]))
+        rope_tables(0)
+        x_words(2)
+        ckv_matmuls(1)
 
-        for b in range(BLOCKS + 1):
+        for b in range(BLOCKS):
+            v_block(b)
+            k_products(b, range(0, 4))
             if b + 1 < BLOCKS:
-                ckv_matmuls(b + 1)
-            if b < BLOCKS:
-                k_products(b)
-            if b + 2 < BLOCKS:
-                x_words(b + 2)
-            if b + 1 < BLOCKS:
-                rope_tables(b + 1)
                 ckv_regroup(b + 1)
             if b + 2 < BLOCKS:
                 x_quantise(b + 2)
@@ -302,5 +321,11 @@ def tile_selfattention_pa_t_kernel(
                 ckv_quantise(b + 1)
             if b >= 1:
                 k_back(b - 1)
-            if b < BLOCKS:
-                v_block(b)
+            if b + 1 < BLOCKS:
+                rope_tables(b + 1)
+            if b + 3 < BLOCKS:
+                x_words(b + 3)
+            k_products(b, range(4, HEADS))
+            if b + 2 < BLOCKS:
+                ckv_matmuls(b + 2)
+        k_back(BLOCKS - 1)

@@ -46,7 +46,7 @@ def tile_selfattention_pa_t_kernel(
         x_dram = x.rearrange("(p t) d -> p t d", t=TILES)
         cos_dram = rope_cos.rearrange("(p t) j -> p t j", t=TILES)
         sin_dram = rope_sin.rearrange("(p t) j -> p t j", t=TILES)
-        k_dram = out_0.rearrange("(p t) h j -> p (t h j)", t=TILES)
+        k_dram = out_0.rearrange("(p t) h j -> p t (h j)", t=TILES)
         v_dram = out_1.rearrange("(p t) h j -> p (t h j)", t=TILES)
 
         x_rows = rows.tile([P, TILES, K], BF16)
@@ -99,6 +99,9 @@ def tile_selfattention_pa_t_kernel(
         swap_f32 = consts.tile([P, P], F32)
         nc.vector.tensor_copy(out=swap_f32[:, 0:HALF], in_=ident_f32[:, HALF:HEAD])
         nc.vector.tensor_copy(out=swap_f32[:, HALF:HEAD], in_=ident_f32[:, 0:HALF])
+        bkv_col = consts.tile([P, 4], F32)
+        bk_col = consts.tile([P, HEADS], F32)
+        bv_twice = consts.tile([P, 2, E], F32)
         for b in range(BLOCKS):
             nc.gpsimd.tensor_scalar(
                 out=sin_rot[:, tiles_of(b), 0:HALF], in0=sin_rows[:, tiles_of(b), HALF:HEAD],
@@ -108,9 +111,11 @@ def tile_selfattention_pa_t_kernel(
                 out=sin_rot[:, tiles_of(b), HALF:HEAD], in0=sin_rows[:, tiles_of(b), 0:HALF],
                 scalar1=-1.0, scalar2=0.0, op0=MULT, op1=ADD,
             )
-        bkv_col = consts.tile([P, 4], F32)
-        bk_col = consts.tile([P, HEADS], F32)
-        bv_twice = consts.tile([P, 2, E], F32)
+            if b == 0:
+                nc.gpsimd.tensor_scalar(
+                    out=bv_twice[:], in0=bv_bf[:].unsqueeze(1).to_broadcast([P, 2, E]),
+                    scalar1=1.0, scalar2=0.0, op0=MULT, op1=ADD,
+                )
 
         down_codes = weights.tile([P, K], U32, align_bytes=64)
         down_scales = weights.tile([P, K], U8, align_bytes=64)
@@ -144,6 +149,7 @@ def tile_selfattention_pa_t_kernel(
         c_mx = {}
         tables = {}
         products = {}
+        k_outs = {}
 
         def x_words(b):
             x_grouped[b] = words_to_partitions(x_rows[:, tiles_of(b), :], s_banks, nc.scalar.copy)
@@ -224,11 +230,13 @@ def tile_selfattention_pa_t_kernel(
                     op1=MULT,
                 )
 
-        def k_back(b):
+        def k_back(b, heads):
             product = products[b]
-            k_out = pairs.tile([P, BLOCK_OUT], F32)
-            by_head = k_out[:].rearrange("p (i h j) -> p i h j", h=HEADS, j=HEAD)
-            for h in range(HEADS):
+            if b not in k_outs:
+                k_out = pairs.tile([P, BLOCK_TILES, HEADS, HEAD], F32)
+                k_outs[b] = k_out
+            k_out = k_outs[b]
+            for h in heads:
                 bank = s_banks.tile([P, BLOCK_TILES, HEAD], F32, tag="bank")
                 for i in range(BLOCK_TILES):
                     toks = slice(i * P, (i + 1) * P)
@@ -240,8 +248,12 @@ def tile_selfattention_pa_t_kernel(
                         out=bank[:, i, :], lhsT=product[:, h, 1, toks], rhs=swap_f32[:],
                         is_transpose=True, start=False, stop=True,
                     )
-                nc.scalar.copy(out=by_head[:, :, h, :], in_=bank[:])
-            nc.sync.dma_start(out=k_dram[:, b * BLOCK_OUT : (b + 1) * BLOCK_OUT], in_=k_out[:])
+                nc.scalar.copy(out=k_out[:, :, h, :], in_=bank[:])
+            cols = slice(heads[0] * HEAD, (heads[-1] + 1) * HEAD)
+            nc.sync.dma_start(
+                out=k_dram[:, tiles_of(b), cols],
+                in_=k_out[:].rearrange("p i h j -> p i (h j)")[:, :, cols],
+            )
 
         def v_block(b):
             c_codes, c_scales = c_mx[b]
@@ -305,14 +317,15 @@ def tile_selfattention_pa_t_kernel(
         ckv_quantise(0)
         up_weights(2, s_banks, nc.scalar.copy)
         nc.vector.tensor_copy(out=bk_col[:], in_=bk_bf[:])
-        nc.vector.tensor_copy(out=bv_twice[:], in_=bv_bf[:].unsqueeze(1).to_broadcast([P, 2, E]))
         rope_tables(0)
         x_words(2)
         ckv_matmuls(1)
 
+        first_heads = range(0, 4)
+        last_heads = range(4, HEADS)
         for b in range(BLOCKS):
             v_block(b)
-            k_products(b, range(0, 4))
+            k_products(b, first_heads)
             if b + 1 < BLOCKS:
                 ckv_regroup(b + 1)
             if b + 2 < BLOCKS:
@@ -320,12 +333,13 @@ def tile_selfattention_pa_t_kernel(
             if b + 1 < BLOCKS:
                 ckv_quantise(b + 1)
             if b >= 1:
-                k_back(b - 1)
+                k_back(b - 1, last_heads)
             if b + 1 < BLOCKS:
                 rope_tables(b + 1)
             if b + 3 < BLOCKS:
                 x_words(b + 3)
-            k_products(b, range(4, HEADS))
+            k_back(b, first_heads)
+            k_products(b, last_heads)
             if b + 2 < BLOCKS:
                 ckv_matmuls(b + 2)
-        k_back(BLOCKS - 1)
+        k_back(BLOCKS - 1, last_heads)

@@ -150,6 +150,7 @@ def tile_selfattention_pa_t_kernel(
         tables = {}
         products = {}
         k_outs = {}
+        v_outs = {}
 
         def x_words(b):
             x_grouped[b] = words_to_partitions(x_rows[:, tiles_of(b), :], s_banks, nc.scalar.copy)
@@ -160,10 +161,13 @@ def tile_selfattention_pa_t_kernel(
             quantise(x_grouped[b], x_codes[:], x_scales[:])
             x_mx[b] = (x_codes, x_scales)
 
-        def ckv_matmuls(b):
+        def ckv_matmuls(b, which):
             x_codes, x_scales = x_mx[b]
-            planes = pairs.tile([P, 4, BLOCK], BF16)
-            for t in range(4):
+            if b not in c_planes:
+                planes = pairs.tile([P, 4, BLOCK], BF16)
+                c_planes[b] = planes
+            planes = c_planes[b]
+            for t in which:
                 cols = slice(t * P, (t + 1) * P)
                 bank = s_banks.tile([P, BLOCK], F32, tag="bank")
                 nc.tensor.matmul_mx(
@@ -178,7 +182,6 @@ def tile_selfattention_pa_t_kernel(
                 nc.scalar.activation(
                     out=planes[:, t, :], in_=bank[:], func=IDENTITY, bias=bkv_col[:, t : t + 1], scale=1.0
                 )
-            c_planes[b] = planes
 
         def ckv_regroup(b):
             grouped = stage.tile([P, 4 * BLOCK], BF16, align_bytes=64)
@@ -249,17 +252,19 @@ def tile_selfattention_pa_t_kernel(
                         is_transpose=True, start=False, stop=True,
                     )
                 nc.scalar.copy(out=k_out[:, :, h, :], in_=bank[:])
-            cols = slice(heads[0] * HEAD, (heads[-1] + 1) * HEAD)
-            nc.sync.dma_start(
-                out=k_dram[:, tiles_of(b), cols],
-                in_=k_out[:].rearrange("p i h j -> p i (h j)")[:, :, cols],
-            )
+            if heads[-1] == HEADS - 1:
+                nc.sync.dma_start(
+                    out=k_dram[:, tiles_of(b), :], in_=k_out[:].rearrange("p i h j -> p i (h j)")
+                )
 
-        def v_block(b):
+        def v_banks_of(b, which):
             c_codes, c_scales = c_mx[b]
-            v_out = pairs.tile([P, BLOCK_OUT], F32)
+            if b not in v_outs:
+                v_out = pairs.tile([P, BLOCK_OUT], F32)
+                v_outs[b] = v_out
+            v_out = v_outs[b]
             bias = bv_twice[:].rearrange("p r e -> p (r e)")
-            for q in range(BLOCK_OUT // BANK):
+            for q in which:
                 on_vector = q % 3 == 0
                 bank = (v_banks if on_vector else s_banks).tile([P, BANK], F32, tag="bank")
                 col = q * BANK
@@ -310,7 +315,7 @@ def tile_selfattention_pa_t_kernel(
         x_quantise(0)
         x_words(1)
         up_weights(0, v_banks, nc.vector.tensor_copy)
-        ckv_matmuls(0)
+        ckv_matmuls(0, range(4))
         up_weights(1, v_banks, nc.vector.tensor_copy)
         ckv_regroup(0)
         x_quantise(1)
@@ -319,27 +324,28 @@ def tile_selfattention_pa_t_kernel(
         nc.vector.tensor_copy(out=bk_col[:], in_=bk_bf[:])
         rope_tables(0)
         x_words(2)
-        ckv_matmuls(1)
+        ckv_matmuls(1, range(4))
 
-        first_heads = range(0, 4)
-        last_heads = range(4, HEADS)
         for b in range(BLOCKS):
-            v_block(b)
-            k_products(b, first_heads)
+            k_products(b, range(0, 4))
+            if b >= 1:
+                k_back(b - 1, range(4, 6))
+            v_banks_of(b, range(0, 3))
             if b + 1 < BLOCKS:
                 ckv_regroup(b + 1)
             if b + 2 < BLOCKS:
                 x_quantise(b + 2)
             if b + 1 < BLOCKS:
                 ckv_quantise(b + 1)
-            if b >= 1:
-                k_back(b - 1, last_heads)
-            if b + 1 < BLOCKS:
                 rope_tables(b + 1)
             if b + 3 < BLOCKS:
                 x_words(b + 3)
-            k_back(b, first_heads)
-            k_products(b, last_heads)
+            v_banks_of(b, range(3, 6))
+            k_back(b, range(0, 2))
+            k_products(b, range(4, 6))
             if b + 2 < BLOCKS:
-                ckv_matmuls(b + 2)
-        k_back(BLOCKS - 1, last_heads)
+                ckv_matmuls(b + 2, range(0, 2))
+            k_back(b, range(2, 4))
+            if b + 2 < BLOCKS:
+                ckv_matmuls(b + 2, range(2, 4))
+        k_back(BLOCKS - 1, range(4, 6))

from contextlib import ExitStack

import concourse.mybir as mybir
from concourse.masks import make_identity

F32 = mybir.dt.float32
BF16 = mybir.dt.bfloat16
U32 = mybir.dt.uint32
U8 = mybir.dt.uint8
FP8X4 = mybir.dt.float8_e4m3fn_x4
ADD = mybir.AluOpType.add
MULT = mybir.AluOpType.mult
IDENTITY = mybir.ActivationFunctionType.Identity

P = 128
TOKENS = 4096
K = 512
HEADS = 6
HEAD = 128
HALF = HEAD // 2
E = HEADS * HEAD
BANK = 512
TILES = TOKENS // P
BLOCK_TILES = 4
BLOCK = BLOCK_TILES * P
BLOCKS = TILES // BLOCK_TILES
BLOCK_OUT = BLOCK_TILES * E

FLOPS = 2 * TOKENS * K * (K + 2 * E)


def tile_selfattention_pa_t_kernel(
    tc, x, rope_cos, rope_sin, wkv_down, bkv_down, wk_up, bk_up, wv_up, bv_up, out_0, out_1
):
    nc = tc.nc
    with ExitStack() as stack:
        consts = stack.enter_context(tc.tile_pool(name="consts", bufs=1))
        rows = stack.enter_context(tc.tile_pool(name="rows", bufs=1))
        weights = stack.enter_context(tc.tile_pool(name="weights", bufs=1))
        stage = stack.enter_context(tc.tile_pool(name="stage", bufs=3))
        pairs = stack.enter_context(tc.tile_pool(name="pairs", bufs=2))
        s_banks = stack.enter_context(tc.psum_pool(name="s_banks", bufs=4))
        v_banks = stack.enter_context(tc.psum_pool(name="v_banks", bufs=4))
        stack.enter_context(tc.manual_schedule())

        x_dram = x.rearrange("(p t) d -> p t d", t=TILES)
        cos_dram = rope_cos.rearrange("(p t) j -> p t j", t=TILES)
        sin_dram = rope_sin.rearrange("(p t) j -> p t j", t=TILES)
        k_dram = out_0.rearrange("(p t) h j -> p t (h j)", t=TILES)
        v_dram = out_1.rearrange("(p t) h j -> p (t h j)", t=TILES)

        x_rows = rows.tile([P, TILES, K], BF16)
        cos_rows = rows.tile([P, TILES, HEAD], BF16)
        sin_rows = rows.tile([P, TILES, HEAD], BF16)
        sin_rot = rows.tile([P, TILES, HEAD], BF16)
        down_rows = rows.tile([P, 4, K], BF16)
        up_rows = rows.tile([P, 2 * HEADS, K], BF16)
        bkv_bf = consts.tile([P, 4], BF16)
        bk_bf = consts.tile([P, HEADS], BF16)
        bv_bf = consts.tile([P, E], BF16)

        def tiles_of(b):
            return slice(b * BLOCK_TILES, (b + 1) * BLOCK_TILES)

        def load_x(b):
            nc.sync.dma_start(out=x_rows[:, tiles_of(b), :], in_=x_dram[:, tiles_of(b), :])

        def load_rope(b):
            nc.sync.dma_start(out=cos_rows[:, tiles_of(b), :], in_=cos_dram[:, tiles_of(b), :])
            nc.sync.dma_start(out=sin_rows[:, tiles_of(b), :], in_=sin_dram[:, tiles_of(b), :])

        nc.sync.dma_start(
            out=down_rows[:].rearrange("m (u e) d -> m u (e d)", u=2),
            in_=wkv_down.rearrange("(u m e) d -> m u (e d)", u=2, e=2),
        )
        load_x(0)
        load_x(1)
        nc.sync.dma_start(
            out=bkv_bf[:].rearrange("m (u e) -> m u e", u=2),
            in_=bkv_down.rearrange("(u m e) -> m u e", u=2, e=2),
        )
        nc.sync.dma_start(out=up_rows[:, 0:HEADS, :], in_=wk_up.rearrange("(a m) c -> m a c", m=P))
        nc.sync.dma_start(
            out=up_rows[:, HEADS : 2 * HEADS, :], in_=wv_up.rearrange("(a m) c -> m a c", m=P)
        )
        load_rope(0)
        with nc.allow_non_contiguous_dma(reason="768 bias values, one head to a column"):
            nc.sync.dma_start(out=bk_bf[:], in_=bk_up.rearrange("(h m) -> m h", m=P))
        nc.sync.dma_start(out=bv_bf[:], in_=bv_up.partition_broadcast(P))
        for b in range(2, BLOCKS):
            load_x(b)
            load_rope(b - 1)
        load_rope(BLOCKS - 1)

        ident_f32 = consts.tile([P, P], F32)
        make_identity(nc, ident_f32[:])
        ident_bf = consts.tile([P, P], BF16)
        make_identity(nc, ident_bf[:])
        swap_f32 = consts.tile([P, P], F32)
        nc.vector.tensor_copy(out=swap_f32[:, 0:HALF], in_=ident_f32[:, HALF:HEAD])
        nc.vector.tensor_copy(out=swap_f32[:, HALF:HEAD], in_=ident_f32[:, 0:HALF])
        bkv_col = consts.tile([P, 4], F32)
        bk_col = consts.tile([P, HEADS], F32)
        bv_twice = consts.tile([P, 2, E], F32)
        for b in range(BLOCKS):
            nc.gpsimd.tensor_scalar(
                out=sin_rot[:, tiles_of(b), 0:HALF], in0=sin_rows[:, tiles_of(b), HALF:HEAD],
                scalar1=1.0, scalar2=0.0, op0=MULT, op1=ADD,
            )
            nc.gpsimd.tensor_scalar(
                out=sin_rot[:, tiles_of(b), HALF:HEAD], in0=sin_rows[:, tiles_of(b), 0:HALF],
                scalar1=-1.0, scalar2=0.0, op0=MULT, op1=ADD,
            )
            if b == 0:
                nc.gpsimd.tensor_scalar(
                    out=bv_twice[:], in0=bv_bf[:].unsqueeze(1).to_broadcast([P, 2, E]),
                    scalar1=1.0, scalar2=0.0, op0=MULT, op1=ADD,
                )

        down_codes = weights.tile([P, K], U32, align_bytes=64)
        down_scales = weights.tile([P, K], U8, align_bytes=64)
        up_codes = weights.tile([P, 2 * E], U32, align_bytes=64)
        up_scales = weights.tile([P, 2 * E], U8, align_bytes=64)

        def words_to_partitions(four_tiles, banks, copy):
            grouped = stage.tile([P, 4 * BLOCK], BF16, align_bytes=64)
            words_in = four_tiles.bitcast(F32)
            words_out = grouped[:].bitcast(F32).rearrange("p (r n u) -> p r n u", r=4, u=2)
            for first in (0, 2):
                bank = banks.tile([P, 2, 2, P], F32, tag="bank")
                for r in range(2):
                    for u in range(2):
                        nc.tensor.transpose(
                            bank[:, r, u, :], words_in[:, first + r, u * P : (u + 1) * P], ident_f32[:]
                        )
                copy(
                    out=words_out[:, first : first + 2, :, :],
                    in_=bank[:].rearrange("p r u n -> p r n u"),
                )
            return grouped

        def quantise(grouped, codes, scales):
            nc.vector.quantize_mx(out=codes.bitcast(FP8X4), scales=scales, in_=grouped[:])

        x_grouped = {}
        x_mx = {}
        c_planes = {}
        c_grouped = {}
        c_mx = {}
        tables = {}
        products = {}
        k_outs = {}
        v_outs = {}

        def x_words(b):
            x_grouped[b] = words_to_partitions(x_rows[:, tiles_of(b), :], s_banks, nc.scalar.copy)

        def x_quantise(b):
            x_codes = pairs.tile([P, BLOCK], U32, align_bytes=64)
            x_scales = pairs.tile([P, BLOCK], U8, align_bytes=64)
            quantise(x_grouped[b], x_codes[:], x_scales[:])
            x_mx[b] = (x_codes, x_scales)

        def ckv_matmuls(b, which):
            x_codes, x_scales = x_mx[b]
            if b not in c_planes:
                planes = pairs.tile([P, 4, BLOCK], BF16)
                c_planes[b] = planes
            planes = c_planes[b]
            for t in which:
                cols = slice(t * P, (t + 1) * P)
                bank = s_banks.tile([P, BLOCK], F32, tag="bank")
                nc.tensor.matmul_mx(
                    out=bank[:],
                    lhsT=down_codes[:, cols].bitcast(FP8X4),
                    lhsT_scale=down_scales[:, cols],
                    rhs=x_codes[:].bitcast(FP8X4),
                    rhs_scale=x_scales[:],
                    start=True,
                    stop=True,
                )
                nc.scalar.activation(
                    out=planes[:, t, :], in_=bank[:], func=IDENTITY, bias=bkv_col[:, t : t + 1], scale=1.0
                )

        def ckv_regroup(b):
            grouped = stage.tile([P, 4 * BLOCK], BF16, align_bytes=64)
            nc.vector.tensor_copy(
                out=grouped[:].rearrange("p (c i t) -> p c t i", i=4, t=4),
                in_=c_planes[b][:].rearrange("p t (c i) -> p c t i", i=4),
            )
            c_grouped[b] = grouped

        def ckv_quantise(b):
            c_codes = pairs.tile([P, BLOCK], U32, align_bytes=64)
            c_scales = pairs.tile([P, BLOCK], U8, align_bytes=64)
            quantise(c_grouped[b], c_codes[:], c_scales[:])
            c_mx[b] = (c_codes, c_scales)

        def rope_tables(b):
            bank = s_banks.tile([P, 2, BLOCK_TILES, P], BF16, tag="bank")
            for i in range(BLOCK_TILES):
                nc.tensor.transpose(bank[:, 0, i, :], cos_rows[:, b * BLOCK_TILES + i, :], ident_bf[:])
                nc.tensor.transpose(bank[:, 1, i, :], sin_rot[:, b * BLOCK_TILES + i, :], ident_bf[:])
            table = pairs.tile([P, 2, BLOCK], BF16)
            nc.scalar.copy(out=table[:], in_=bank[:].rearrange("p w i n -> p w (i n)"))
            tables[b] = table

        def k_products(b, heads):
            c_codes, c_scales = c_mx[b]
            if b not in products:
                product = pairs.tile([P, HEADS, 2, BLOCK], F32)
                products[b] = product
            product = products[b]
            for h in heads:
                cols = slice(h * HEAD, (h + 1) * HEAD)
                bank = v_banks.tile([P, BLOCK], F32, tag="bank")
                nc.tensor.matmul_mx(
                    out=bank[:],
                    lhsT=up_codes[:, cols].bitcast(FP8X4),
                    lhsT_scale=up_scales[:, cols],
                    rhs=c_codes[:].bitcast(FP8X4),
                    rhs_scale=c_scales[:],
                    start=True,
                    stop=True,
                )
                nc.vector.scalar_tensor_tensor(
                    out=product[:, h, :, :],
                    in0=bank[:].unsqueeze(1).to_broadcast([P, 2, BLOCK]),
                    scalar=bk_col[:, h : h + 1],
                    in1=tables[b][:],
                    op0=ADD,
                    op1=MULT,
                )

        def k_back(b, heads):
            product = products[b]
            if b not in k_outs:
                k_out = pairs.tile([P, BLOCK_TILES, HEADS, HEAD], F32)
                k_outs[b] = k_out
            k_out = k_outs[b]
            for h in heads:
                bank = s_banks.tile([P, BLOCK_TILES, HEAD], F32, tag="bank")
                for i in range(BLOCK_TILES):
                    toks = slice(i * P, (i + 1) * P)
                    nc.tensor.matmul(
                        out=bank[:, i, :], lhsT=product[:, h, 0, toks], rhs=ident_f32[:],
                        is_transpose=True, start=True, stop=False,
                    )
                    nc.tensor.matmul(
                        out=bank[:, i, :], lhsT=product[:, h, 1, toks], rhs=swap_f32[:],
                        is_transpose=True, start=False, stop=True,
                    )
                nc.scalar.copy(out=k_out[:, :, h, :], in_=bank[:])
            if heads[-1] == HEADS - 1:
                nc.sync.dma_start(
                    out=k_dram[:, tiles_of(b), :], in_=k_out[:].rearrange("p i h j -> p i (h j)")
                )

        def v_banks_of(b, which):
            c_codes, c_scales = c_mx[b]
            if b not in v_outs:
                v_out = pairs.tile([P, BLOCK_OUT], F32)
                v_outs[b] = v_out
            v_out = v_outs[b]
            bias = bv_twice[:].rearrange("p r e -> p (r e)")
            for q in which:
                on_vector = q % 3 == 0
                bank = (v_banks if on_vector else s_banks).tile([P, BANK], F32, tag="bank")
                col = q * BANK
                while col < (q + 1) * BANK:
                    i, e0 = divmod(col, E)
                    width = min(E - e0, (q + 1) * BANK - col)
                    toks = slice(i * P, (i + 1) * P)
                    w_cols = slice(E + e0, E + e0 + width)
                    nc.tensor.matmul_mx(
                        out=bank[:, col - q * BANK : col - q * BANK + width],
                        lhsT=c_codes[:, toks].bitcast(FP8X4),
                        lhsT_scale=c_scales[:, toks],
                        rhs=up_codes[:, w_cols].bitcast(FP8X4),
                        rhs_scale=up_scales[:, w_cols],
                        start=True,
                        stop=True,
                    )
                    col += width
                if on_vector:
                    nc.vector.tensor_tensor(
                        out=v_out[:, q * BANK : (q + 1) * BANK], in0=bank[:], in1=bias[:, 0:BANK], op=ADD
                    )
                else:
                    nc.scalar.copy(out=v_out[:, q * BANK : (q + 1) * BANK], in_=bank[:])
                if q % 3 == 2:
                    two_banks = slice((q - 1) * BANK, (q + 1) * BANK)
                    nc.gpsimd.tensor_tensor(
                        out=v_out[:, two_banks], in0=v_out[:, two_banks], in1=bias[:, BANK : 3 * BANK], op=ADD
                    )
                    three_banks = slice((q - 2) * BANK, (q + 1) * BANK)
                    nc.sync.dma_start(
                        out=v_dram[:, b * BLOCK_OUT + (q - 2) * BANK : b * BLOCK_OUT + (q + 1) * BANK],
                        in_=v_out[:, three_banks],
                    )

        def down_weights():
            grouped = words_to_partitions(down_rows[:], v_banks, nc.vector.tensor_copy)
            quantise(grouped, down_codes[:], down_scales[:])
            nc.vector.tensor_copy(out=bkv_col[:], in_=bkv_bf[:])

        def up_weights(chunk, banks, copy):
            grouped = words_to_partitions(up_rows[:, 4 * chunk : 4 * chunk + 4, :], banks, copy)
            cols = slice(chunk * BLOCK, (chunk + 1) * BLOCK)
            quantise(grouped, up_codes[:, cols], up_scales[:, cols])

        down_weights()
        x_words(0)
        x_quantise(0)
        x_words(1)
        up_weights(0, v_banks, nc.vector.tensor_copy)
        ckv_matmuls(0, range(4))
        up_weights(1, v_banks, nc.vector.tensor_copy)
        ckv_regroup(0)
        x_quantise(1)
        ckv_quantise(0)
        up_weights(2, s_banks, nc.scalar.copy)
        nc.vector.tensor_copy(out=bk_col[:], in_=bk_bf[:])
        rope_tables(0)
        x_words(2)
        ckv_matmuls(1, range(4))

        for b in range(BLOCKS):
            k_products(b, range(0, 4))
            if b >= 1:
                k_back(b - 1, range(4, 6))
            v_banks_of(b, range(0, 3))
            if b + 1 < BLOCKS:
                ckv_regroup(b + 1)
            if b + 2 < BLOCKS:
                x_quantise(b + 2)
            if b + 1 < BLOCKS:
                ckv_quantise(b + 1)
                rope_tables(b + 1)
            if b + 3 < BLOCKS:
                x_words(b + 3)
            v_banks_of(b, range(3, 6))
            k_back(b, range(0, 2))
            k_products(b, range(4, 6))
            if b + 2 < BLOCKS:
                ckv_matmuls(b + 2, range(0, 2))
            k_back(b, range(2, 4))
            if b + 2 < BLOCKS:
                ckv_matmuls(b + 2, range(2, 4))
        k_back(BLOCKS - 1, range(4, 6))
